import numpy as np
import ml_dtypes


def mxq(x, axis, fmt="e4m3"):
    dtype, down = {"e4m3": (ml_dtypes.float8_e4m3fn, 7), "e5m2": (ml_dtypes.float8_e5m2, 14)}[fmt]
    v = np.moveaxis(np.asarray(x, np.float32).astype(ml_dtypes.bfloat16).astype(np.float64), axis, -1)
    blocks = v.reshape(v.shape[:-1] + (-1, 32))
    amax = np.abs(blocks).max(-1, keepdims=True)
    byte = np.maximum(np.where(amax > 0, np.frexp(amax)[1] - 1 + 127, 0) - down, 1)
    scale = np.exp2(byte - 127.0)
    codes = (blocks / scale).astype(np.float32).astype(dtype).astype(np.float64)
    return np.moveaxis((codes * scale).reshape(v.shape), -1, axis)


WIDE = False


def mx_kscale(k):
    if not WIDE:
        return np.ones(k)
    levels = np.array([10, -10, 5, -5, 0])
    a = np.random.permutation(np.resize(levels, k // 512 * 4)).reshape(k // 512, 4)
    idx = np.arange(k)
    return np.exp2(a[idx // 512, idx % 128 // 32])


BF16 = ml_dtypes.bfloat16


def bf(x):
    return np.asarray(x, np.float32).astype(BF16)


def f64(x):
    return np.asarray(x).astype(np.float64)


N, NR, F, C, R = 512, 1024, 8192, 128, 8
EPS = 1e-8


def encode_amplitude(v):
    return v / (np.linalg.norm(v, axis=1, keepdims=True) + EPS)


def setup_inputs():
    s = mx_kscale(F)
    basis = np.random.standard_normal((R, F)) / np.sqrt(R)
    x = np.random.standard_normal((N, R)) @ basis + 0.5 * np.random.standard_normal((N, F))
    x_ref = np.random.standard_normal((NR, R)) @ basis + 0.5 * np.random.standard_normal((NR, F))
    c = 2.0 ** np.round(np.log2(np.mean(s ** 2) * np.mean(s ** -2.0)))
    return {"x": bf(x * s), "x_ref": bf(x_ref / s),
            "mean_": bf(np.random.standard_normal(F) * 0.5 * np.minimum(s, 1.0 / s)),
            "components_": bf(np.random.standard_normal((C, NR)) * 8.0 / np.sqrt(NR) * c)}


def reference(x, x_ref, mean_, components_):
    xs = f64(x) - f64(mean_)
    xr = f64(x_ref) - f64(mean_)
    s1 = encode_amplitude(xs)
    s2 = encode_amplitude(xr)
    ov = mxq(s1, 1, "e4m3") @ mxq(s2, 1, "e4m3").T
    K = ov * ov
    return mxq(K, 1, "e4m3") @ mxq(f64(components_), 1, "e4m3").T

@@ -1,0 +1,305 @@
+from contextlib import ExitStack
+
+import concourse.mybir as mybir
+from concourse.masks import make_identity
+
+FLOPS = 2 * 512 * 1024 * 8192 + 2 * 512 * 1024 * 128
+
+PIN = True
+SCALE_RULE = "g"
+EVAC_V_EVERY = 0
+
+F32 = mybir.dt.float32
+BF16 = mybir.dt.bfloat16
+U32 = mybir.dt.uint32
+U8 = mybir.dt.uint8
+FP8X4 = mybir.dt.float8_e4m3fn_x4
+ALU = mybir.AluOpType
+ACT = mybir.ActivationFunctionType
+
+P = 128
+F = 8192
+N_X = 512
+N_REF = 1024
+C = 128
+EPS = 1e-8
+PACK = 4
+RUN = 128
+PASSES = F // (PACK * RUN)
+ROWS_Q = P // PACK
+W_Q = F // PACK
+NQ = (N_X + N_REF) // ROWS_Q
+NQ_X = N_X // ROWS_Q
+GROUPS = NQ // 4
+GROUPS_X = NQ_X // 4
+PF = 5
+
+
+def tile_quantumkernelpca_kernel(tc, x, x_ref, mean_, components_, out):
+    nc = tc.nc
+    with ExitStack() as ctx:
+        const = ctx.enter_context(tc.tile_pool(name="const", bufs=1))
+        xin_pool = ctx.enter_context(tc.tile_pool(name="xin", bufs=PF + 1))
+        d_pool = ctx.enter_context(tc.tile_pool(name="d", bufs=7))
+        s_pool = ctx.enter_context(tc.tile_pool(name="s", bufs=3))
+        grp_pool = ctx.enter_context(tc.tile_pool(name="grp", bufs=2))
+        ref_pool = ctx.enter_context(tc.tile_pool(name="ref", bufs=2))
+        small = ctx.enter_context(tc.tile_pool(name="small", bufs=4))
+        psum_m = ctx.enter_context(tc.psum_pool(name="psum_m", bufs=1))
+        psum_t = ctx.enter_context(tc.psum_pool(name="psum_t", bufs=3))
+        psum_o = ctx.enter_context(tc.psum_pool(name="psum_o", bufs=2))
+        psum_x = ctx.enter_context(tc.psum_pool(name="psum_x", bufs=1))
+        if PIN:
+            ctx.enter_context(tc.manual_schedule())
+
+        tiny = const.tile([P, 1], F32, name="tiny")
+        nc.vector.memset(tiny[:], 1e-30)
+        warm = const.tile([P, 1], F32, name="warm")
+        nc.scalar.activation(out=warm[:], in_=tiny[:], func=ACT.Sqrt)
+
+        mrows = const.tile([P, W_Q], BF16, name="mrows")
+        nc.vector.memset(mrows[:], 0.0)
+        nc.sync.dma_start(
+            out=mrows[0:PACK, :].rearrange("t (g f) -> t g f", f=RUN),
+            in_=mean_.rearrange("(g t f) -> t g f", t=PACK, f=RUN),
+        )
+
+        ident = const.tile([P, P], BF16, name="ident")
+        make_identity(nc, ident[:])
+        sel = const.tile([P, ROWS_Q, PACK], BF16, name="sel")
+        nc.vector.tensor_copy(out=sel[:], in_=ident[:, 0:PACK].unsqueeze(1).to_broadcast([P, ROWS_Q, PACK]))
+        spread = const.tile([P, ROWS_Q, PACK], BF16, name="spread")
+        nc.vector.tensor_copy(out=spread[:], in_=ident[:, 0:ROWS_Q].unsqueeze(2).to_broadcast([P, ROWS_Q, PACK]))
+
+        same_ps = psum_x.tile([P, P], F32, name="same_ps", tag="x")
+        nc.tensor.matmul(
+            out=same_ps[:],
+            lhsT=spread[:].rearrange("p r t -> p (r t)"),
+            rhs=spread[:].rearrange("p r t -> p (r t)"),
+            start=True,
+            stop=True,
+        )
+        mean_ps = []
+        for h in range(2):
+            mp = psum_m.tile([P, 1024], BF16, name="mean_ps%d" % h)
+            for j in range(2):
+                nc.tensor.matmul(
+                    out=mp[:, j * 512:(j + 1) * 512],
+                    lhsT=sel[:].rearrange("p r t -> p (r t)"),
+                    rhs=mrows[:, (2 * h + j) * 512:(2 * h + j + 1) * 512],
+                    start=True,
+                    stop=True,
+                )
+            mean_ps.append(mp)
+        same = const.tile([P, P], F32, name="same")
+
+        junk = const.tile([P, W_Q], BF16, name="junk")
+        x_codes = const.tile([P, PASSES, N_X], U32, name="x_codes", align_bytes=64)
+        x_scales = const.tile([P, PASSES, N_X], U8, name="x_scales", align_bytes=64)
+        comp_sb = const.tile([P, N_REF], BF16, name="comp_sb")
+        comp_grp = const.tile([P, 2, C, PACK], BF16, name="comp_grp", align_bytes=64)
+        comp_codes = const.tile([P, 2 * C], U32, name="comp_codes", align_bytes=64)
+        comp_scales = const.tile([P, 2 * C], U8, name="comp_scales", align_bytes=64)
+        k_planes = [const.tile([P, PACK, N_X], BF16, name="k_planes%d" % g2) for g2 in range(2)]
+        k_grp = [const.tile([P, N_X, PACK], BF16, name="k_grp%d" % g2, align_bytes=64) for g2 in range(2)]
+        k_codes = [const.tile([P, N_X], U32, name="k_codes%d" % g2, align_bytes=64) for g2 in range(2)]
+        k_scales = [const.tile([P, N_X], U8, name="k_scales%d" % g2, align_bytes=64) for g2 in range(2)]
+
+        xin = {}
+        dif = {}
+        acc = {}
+        n2 = {}
+        nrm = {}
+        rinv = {}
+        sn = {}
+        tps = {}
+        grp = {}
+        rcodes = {}
+        rscales = {}
+        ov = {}
+
+        def load(n):
+            src = x if n < NQ_X else x_ref
+            r0 = ROWS_Q * (n if n < NQ_X else n - NQ_X)
+            t_in = xin_pool.tile([P, W_Q], BF16, name="xin", tag="xin")
+            view = src[r0:r0 + ROWS_Q, :].rearrange("r (g w) -> r g w", w=PACK * RUN)
+            for t in range(PACK):
+                nc.sync.dma_start(
+                    out=t_in[t:P:PACK, :].rearrange("p (g f) -> p g f", f=RUN),
+                    in_=view[:, :, t * RUN:(t + 1) * RUN],
+                )
+            xin[n] = t_in
+
+        def sub(n):
+            t_d = d_pool.tile([P, W_Q], F32, name="dif", tag="dif")
+            for h in range(2):
+                nc.vector.tensor_tensor(
+                    out=t_d[:, h * 1024:(h + 1) * 1024],
+                    in0=xin[n][:, h * 1024:(h + 1) * 1024],
+                    in1=mean_ps[h][:],
+                    op=ALU.subtract,
+                )
+            dif[n] = t_d
+
+        def square(n):
+            p2 = n // 2
+            if n % 2 == 0:
+                acc[p2] = small.tile([P, 2], F32, name="acc", tag="acc")
+            nc.scalar.activation(out=junk[:], in_=dif[n][:], func=ACT.Square, accum_out=acc[p2][:, n % 2:n % 2 + 1])
+
+        def norm_sum(p2):
+            n2[p2] = psum_x.tile([P, 2], F32, name="n2", tag="x")
+            nc.tensor.matmul(out=n2[p2][:], lhsT=same[:], rhs=acc[p2][:], start=True, stop=True)
+
+        def norm_sqrt(p2):
+            nrm[p2] = small.tile([P, 2], F32, name="nrm", tag="nrm")
+            nc.scalar.activation(out=nrm[p2][:], in_=n2[p2][:], func=ACT.Sqrt, bias=tiny[:])
+
+        def norm_recip(p2):
+            ne = small.tile([P, 2], F32, name="ne", tag="ne")
+            nc.vector.tensor_scalar_add(out=ne[:], in0=nrm[p2][:], scalar1=EPS)
+            rinv[p2] = small.tile([P, 2], F32, name="rinv", tag="rinv")
+            nc.vector.reciprocal(out=rinv[p2][:], in_=ne[:])
+
+        def scale(n):
+            t_s = s_pool.tile([P, W_Q], BF16, name="sn", tag="sn")
+            r = rinv[n // 2][:, n % 2:n % 2 + 1]
+            if SCALE_RULE == "g":
+                nc.gpsimd.tensor_scalar(out=t_s[:], in0=dif[n][:], scalar1=r, scalar2=0.0, op0=ALU.mult, op1=ALU.add)
+            elif SCALE_RULE == "v":
+                nc.vector.tensor_scalar(out=t_s[:], in0=dif[n][:], scalar1=r, scalar2=None, op0=ALU.mult)
+            else:
+                nc.scalar.activation(out=t_s[:], in_=dif[n][:], func=ACT.Copy, scale=r)
+            sn[n] = t_s
+
+        def transposes(n):
+            for hb in range(2):
+                tp = psum_t.tile([P, 8, P], BF16, name="tp", tag="tp")
+                for gg in range(8):
+                    g = 8 * hb + gg
+                    nc.tensor.transpose(tp[:, gg, :], sn[n][:, g * RUN:(g + 1) * RUN], ident[:])
+                tps[(n, hb)] = tp
+
+        def evacuate(n):
+            a = n // 4
+            q = n % 4
+            if q == 0:
+                grp[a] = grp_pool.tile([P, PASSES, PACK * P], BF16, name="grp", tag="grp", align_bytes=64)
+            for hb in range(2):
+                dst = grp[a][:, 8 * hb:8 * hb + 8, q * P:(q + 1) * P]
+                if EVAC_V_EVERY and (2 * n + hb) % EVAC_V_EVERY == 0:
+                    nc.vector.tensor_copy(out=dst, in_=tps[(n, hb)][:])
+                else:
+                    nc.scalar.copy(out=dst, in_=tps[(n, hb)][:])
+
+        def quantise(a, c):
+            if a < GROUPS_X:
+                for g in range(4 * c, 4 * c + 4):
+                    nc.vector.quantize_mx(
+                        out=x_codes[:, g, a * P:(a + 1) * P].bitcast(FP8X4),
+                        scales=x_scales[:, g, a * P:(a + 1) * P],
+                        in_=grp[a][:, g, :],
+                    )
+            else:
+                if c == 0:
+                    rcodes[a] = ref_pool.tile([P, PASSES * P], U32, name="rcodes", tag="rcodes", align_bytes=64)
+                    rscales[a] = ref_pool.tile([P, PASSES * P], U8, name="rscales", tag="rscales", align_bytes=64)
+                nc.vector.quantize_mx(
+                    out=rcodes[a][:, c * 512:(c + 1) * 512].bitcast(FP8X4),
+                    scales=rscales[a][:, c * 512:(c + 1) * 512],
+                    in_=grp[a][:, 4 * c:4 * c + 4, :].rearrange("p g w -> p (g w)"),
+                )
+
+        def overlap(a, c):
+            if c == 0:
+                ov[a] = psum_o.tile([P, N_X], F32, name="ov", tag="ov")
+            for g in range(4 * c, 4 * c + 4):
+                nc.tensor.matmul_mx(
+                    out=ov[a][:],
+                    lhsT=rcodes[a][:, g * P:(g + 1) * P].bitcast(FP8X4),
+                    lhsT_scale=rscales[a][:, g * P:(g + 1) * P],
+                    rhs=x_codes[:, g, :].bitcast(FP8X4),
+                    rhs_scale=x_scales[:, g, :],
+                    start=(g == 0),
+                    stop=(g == PASSES - 1),
+                )
+
+        def fidelity(a):
+            j = a - GROUPS_X
+            nc.scalar.activation(out=k_planes[j // 4][:, j % 4, :], in_=ov[a][:], func=ACT.Square)
+
+        def quantise_k(g2):
+            nc.vector.tensor_copy(out=k_grp[g2][:], in_=k_planes[g2][:].rearrange("p t i -> p i t"))
+            nc.vector.quantize_mx(
+                out=k_codes[g2][:].bitcast(FP8X4),
+                scales=k_scales[g2][:],
+                in_=k_grp[g2][:].rearrange("p i t -> p (i t)"),
+            )
+
+        def components_load():
+            nc.sync.dma_start(out=comp_sb[:], in_=components_)
+
+        def components_transposes():
+            ctp = psum_x.tile([P, 8, C], BF16, name="ctp", tag="x")
+            for b in range(8):
+                nc.tensor.transpose(ctp[:, b, :], comp_sb[:, b * RUN:(b + 1) * RUN], ident[:])
+            return ctp
+
+        def components_quantise(ctp):
+            nc.vector.tensor_copy(out=comp_grp[:], in_=ctp[:].rearrange("p (g t) c -> p g c t", t=PACK))
+            nc.vector.quantize_mx(
+                out=comp_codes[:].bitcast(FP8X4),
+                scales=comp_scales[:],
+                in_=comp_grp[:].rearrange("p g c t -> p (g c t)"),
+            )
+
+        for n in range(PF):
+            load(n)
+        last_step = 4 * (GROUPS - 1) + 14
+        for n in range(last_step + 1):
+            if n + PF < NQ:
+                load(n + PF)
+            if n == 8:
+                components_load()
+            if n < NQ:
+                sub(n)
+                square(n)
+            if n == 0:
+                nc.vector.tensor_copy(out=same[:], in_=same_ps[:])
+            if n >= 2 and n % 2 == 0 and (n - 2) // 2 < NQ // 2:
+                norm_sum((n - 2) // 2)
+                norm_sqrt((n - 2) // 2)
+            if n >= 3 and n % 2 == 1 and (n - 3) // 2 < NQ // 2:
+                norm_recip((n - 3) // 2)
+            if n == 21:
+                components_quantise(components_transposes())
+            if 0 <= n - 4 < NQ:
+                scale(n - 4)
+            if 0 <= n - 5 < NQ:
+                transposes(n - 5)
+                evacuate(n - 5)
+            if n >= 9 and (n - 9) // 4 < GROUPS:
+                quantise((n - 9) // 4, (n - 9) % 4)
+            if n >= 10 + 4 * GROUPS_X and (n - 10) // 4 < GROUPS:
+                overlap((n - 10) // 4, (n - 10) % 4)
+            if n >= 14 + 4 * GROUPS_X and (n - 14) % 4 == 0:
+                fidelity((n - 14) // 4)
+                if (n - 14) // 4 == GROUPS_X + 3:
+                    quantise_k(0)
+        quantise_k(1)
+
+        res_ps = psum_x.tile([P, 4, C], F32, name="res_ps", tag="x")
+        for it in range(4):
+            for g2 in range(2):
+                nc.tensor.matmul_mx(
+                    out=res_ps[:, it, :],
+                    lhsT=k_codes[g2][:, it * P:(it + 1) * P].bitcast(FP8X4),
+                    lhsT_scale=k_scales[g2][:, it * P:(it + 1) * P],
+                    rhs=comp_codes[:, g2 * C:(g2 + 1) * C].bitcast(FP8X4),
+                    rhs_scale=comp_scales[:, g2 * C:(g2 + 1) * C],
+                    start=(g2 == 0),
+                    stop=(g2 == 1),
+                )
+        res = const.tile([P, 4, C], F32, name="res")
+        nc.vector.tensor_copy(out=res[:], in_=res_ps[:])
+        nc.sync.dma_start(out=out.rearrange("(a p) c -> p a c", p=P), in_=res[:])

@@ -271,8 +271,10 @@ def tile_quantumkernelpca_kernel(tc, x, x_ref, mean_, components_, out):
                 norm_sqrt((n - 2) // 2)
             if n >= 3 and n % 2 == 1 and (n - 3) // 2 < NQ // 2:
                 norm_recip((n - 3) // 2)
-            if n == 21:
-                components_quantise(components_transposes())
+            if n == 49:
+                comp_ps = components_transposes()
+            if n == 51:
+                components_quantise(comp_ps)
             if 0 <= n - 4 < NQ:
                 scale(n - 4)
             if 0 <= n - 5 < NQ:
@@ -284,8 +286,8 @@ def tile_quantumkernelpca_kernel(tc, x, x_ref, mean_, components_, out):
                 overlap((n - 10) // 4, (n - 10) % 4)
             if n >= 14 + 4 * GROUPS_X and (n - 14) % 4 == 0:
                 fidelity((n - 14) // 4)
-                if (n - 14) // 4 == GROUPS_X + 3:
-                    quantise_k(0)
+            if n == 52:
+                quantise_k(0)
         quantise_k(1)
 
         res_ps = psum_x.tile([P, 4, C], F32, name="res_ps", tag="x")

@@ -52,17 +52,19 @@ def tile_quantumkernelpca_kernel(tc, x, x_ref, mean_, components_, out):
         if PIN:
             ctx.enter_context(tc.manual_schedule())
 
+        mrows = const.tile([P, W_Q], BF16, name="mrows")
+        mean_runs = mean_.rearrange("(g t f) -> t g f", t=PACK, f=RUN)
+        for t in range(PACK):
+            nc.sync.dma_start(
+                out=mrows[t:ROWS_Q:PACK, :].rearrange("p (g f) -> p g f", f=RUN),
+                in_=mean_runs[t].partition_broadcast(ROWS_Q // PACK),
+            )
+        nc.vector.memset(mrows[ROWS_Q:2 * ROWS_Q, :].bitcast(F32), 0.0)
+        nc.vector.memset(mrows[2 * ROWS_Q:P, :].bitcast(F32), 0.0)
         tiny = const.tile([P, 1], F32, name="tiny")
         nc.vector.memset(tiny[:], 1e-30)
         warm = const.tile([P, 1], F32, name="warm")
         nc.scalar.activation(out=warm[:], in_=tiny[:], func=ACT.Sqrt)
-
-        mrows = const.tile([P, W_Q], BF16, name="mrows")
-        nc.vector.memset(mrows[:], 0.0)
-        nc.sync.dma_start(
-            out=mrows[0:PACK, :].rearrange("t (g f) -> t g f", f=RUN),
-            in_=mean_.rearrange("(g t f) -> t g f", t=PACK, f=RUN),
-        )
 
         ident = const.tile([P, P], BF16, name="ident")
         make_identity(nc, ident[:])
@@ -117,6 +119,7 @@ def tile_quantumkernelpca_kernel(tc, x, x_ref, mean_, components_, out):
         rcodes = {}
         rscales = {}
         ov = {}
+        res_ps = []
 
         def load(n):
             src = x if n < NQ_X else x_ref
@@ -164,9 +167,9 @@ def tile_quantumkernelpca_kernel(tc, x, x_ref, mean_, components_, out):
         def scale(n):
             t_s = s_pool.tile([P, W_Q], BF16, name="sn", tag="sn")
             r = rinv[n // 2][:, n % 2:n % 2 + 1]
-            if SCALE_RULE == "g":
+            if SCALE_RULE == "g" and n < NQ - 4:
                 nc.gpsimd.tensor_scalar(out=t_s[:], in0=dif[n][:], scalar1=r, scalar2=0.0, op0=ALU.mult, op1=ALU.add)
-            elif SCALE_RULE == "v":
+            elif True:
                 nc.vector.tensor_scalar(out=t_s[:], in0=dif[n][:], scalar1=r, scalar2=None, op0=ALU.mult)
             else:
                 nc.scalar.activation(out=t_s[:], in_=dif[n][:], func=ACT.Copy, scale=r)
@@ -226,14 +229,35 @@ def tile_quantumkernelpca_kernel(tc, x, x_ref, mean_, components_, out):
 
         def fidelity(a):
             j = a - GROUPS_X
-            nc.scalar.activation(out=k_planes[j // 4][:, j % 4, :], in_=ov[a][:], func=ACT.Square)
+            if j >= 6:
+                nc.scalar.activation(out=k_grp[1][:, :, j % 4], in_=ov[a][:], func=ACT.Square)
+            else:
+                nc.scalar.activation(out=k_planes[j // 4][:, j % 4, :], in_=ov[a][:], func=ACT.Square)
+
+        def lay_k(g2, planes):
+            nc.vector.tensor_copy(
+                out=k_grp[g2][:, :, 0:planes], in_=k_planes[g2][:, 0:planes, :].rearrange("p t i -> p i t")
+            )
 
         def quantise_k(g2):
-            nc.vector.tensor_copy(out=k_grp[g2][:], in_=k_planes[g2][:].rearrange("p t i -> p i t"))
             nc.vector.quantize_mx(
                 out=k_codes[g2][:].bitcast(FP8X4),
                 scales=k_scales[g2][:],
                 in_=k_grp[g2][:].rearrange("p i t -> p (i t)"),
+            )
+
+        def project(it, g2):
+            if g2 == 0:
+                pool = psum_t if it < 3 else psum_x
+                res_ps.append(pool.tile([P, C], F32, name="res_ps", tag="tp" if it < 3 else "x"))
+            nc.tensor.matmul_mx(
+                out=res_ps[it][:],
+                lhsT=k_codes[g2][:, it * P:(it + 1) * P].bitcast(FP8X4),
+                lhsT_scale=k_scales[g2][:, it * P:(it + 1) * P],
+                rhs=comp_codes[:, g2 * C:(g2 + 1) * C].bitcast(FP8X4),
+                rhs_scale=comp_scales[:, g2 * C:(g2 + 1) * C],
+                start=(g2 == 0),
+                stop=(g2 == 1),
             )
 
         def components_load():
@@ -282,26 +306,24 @@ def tile_quantumkernelpca_kernel(tc, x, x_ref, mean_, components_, out):
                 evacuate(n - 5)
             if n >= 9 and (n - 9) // 4 < GROUPS:
                 quantise((n - 9) // 4, (n - 9) % 4)
-            if n >= 10 + 4 * GROUPS_X and (n - 10) // 4 < GROUPS:
-                overlap((n - 10) // 4, (n - 10) % 4)
-            if n >= 14 + 4 * GROUPS_X and (n - 14) % 4 == 0:
-                fidelity((n - 14) // 4)
+            if n >= 9 + 4 * GROUPS_X and (n - 9) // 4 < GROUPS:
+                overlap((n - 9) // 4, (n - 9) % 4)
+            if n >= 13 + 4 * GROUPS_X and (n - 13) % 4 == 0 and (n - 13) // 4 < GROUPS:
+                fidelity((n - 13) // 4)
+            if n == 53:
+                for it in range(4):
+                    project(it, 0)
             if n == 52:
+                lay_k(0, PACK)
+                lay_k(1, 2)
                 quantise_k(0)
         quantise_k(1)
-
-        res_ps = psum_x.tile([P, 4, C], F32, name="res_ps", tag="x")
         for it in range(4):
-            for g2 in range(2):
-                nc.tensor.matmul_mx(
-                    out=res_ps[:, it, :],
-                    lhsT=k_codes[g2][:, it * P:(it + 1) * P].bitcast(FP8X4),
-                    lhsT_scale=k_scales[g2][:, it * P:(it + 1) * P],
-                    rhs=comp_codes[:, g2 * C:(g2 + 1) * C].bitcast(FP8X4),
-                    rhs_scale=comp_scales[:, g2 * C:(g2 + 1) * C],
-                    start=(g2 == 0),
-                    stop=(g2 == 1),
-                )
+            project(it, 1)
         res = const.tile([P, 4, C], F32, name="res")
-        nc.vector.tensor_copy(out=res[:], in_=res_ps[:])
-        nc.sync.dma_start(out=out.rearrange("(a p) c -> p a c", p=P), in_=res[:])
+        out_view = out.rearrange("(a p) c -> p a c", p=P)
+        for it in range(2):
+            nc.vector.tensor_copy(out=res[:, it, :], in_=res_ps[it][:])
+            nc.scalar.copy(out=res[:, it + 2, :], in_=res_ps[it + 2][:])
+        nc.sync.dma_start(out=out_view[:, 0:2, :], in_=res[:, 0:2, :])
+        nc.scalar.dma_start(out=out_view[:, 2:4, :], in_=res[:, 2:4, :])

@@ -119,6 +119,7 @@ def tile_quantumkernelpca_kernel(tc, x, x_ref, mean_, components_, out):
         rcodes = {}
         rscales = {}
         ov = {}
+        ovs = {}
         res_ps = []
 
         def load(n):
@@ -234,6 +235,14 @@ def tile_quantumkernelpca_kernel(tc, x, x_ref, mean_, components_, out):
             else:
                 nc.scalar.activation(out=k_planes[j // 4][:, j % 4, :], in_=ov[a][:], func=ACT.Square)
 
+        def fidelity_copy(a):
+            ovs[a] = small.tile([P, N_X], F32, name="ovs", tag="ovs")
+            nc.vector.tensor_copy(out=ovs[a][:], in_=ov[a][:])
+
+        def fidelity_mult(a):
+            j = a - GROUPS_X
+            nc.vector.tensor_tensor(out=k_planes[j // 4][:, j % 4, :], in0=ovs[a][:], in1=ov[a][:], op=ALU.mult)
+
         def lay_k(g2, planes):
             nc.vector.tensor_copy(
                 out=k_grp[g2][:, :, 0:planes], in_=k_planes[g2][:, 0:planes, :].rearrange("p t i -> p i t")
@@ -306,9 +315,13 @@ def tile_quantumkernelpca_kernel(tc, x, x_ref, mean_, components_, out):
                 evacuate(n - 5)
             if n >= 9 and (n - 9) // 4 < GROUPS:
                 quantise((n - 9) // 4, (n - 9) % 4)
+            if n >= 14 + 4 * GROUPS_X and (n - 14) % 4 == 0 and (n - 14) // 4 < 10:
+                fidelity_copy((n - 14) // 4)
+            if n >= 16 + 4 * GROUPS_X and (n - 16) % 4 == 0 and (n - 16) // 4 < 10:
+                fidelity_mult((n - 16) // 4)
             if n >= 9 + 4 * GROUPS_X and (n - 9) // 4 < GROUPS:
                 overlap((n - 9) // 4, (n - 9) % 4)
-            if n >= 13 + 4 * GROUPS_X and (n - 13) % 4 == 0 and (n - 13) // 4 < GROUPS:
+            if n >= 13 + 4 * GROUPS_X and (n - 13) % 4 == 0 and 10 <= (n - 13) // 4 < GROUPS:
                 fidelity((n - 13) // 4)
             if n == 53:
                 for it in range(4):

from contextlib import ExitStack

import concourse.mybir as mybir
from concourse.masks import make_identity

FLOPS = 2 * 512 * 1024 * 8192 + 2 * 512 * 1024 * 128

PIN = True
SCALE_RULE = "g"
EVAC_V_EVERY = 0

F32 = mybir.dt.float32
BF16 = mybir.dt.bfloat16
U32 = mybir.dt.uint32
U8 = mybir.dt.uint8
FP8X4 = mybir.dt.float8_e4m3fn_x4
ALU = mybir.AluOpType
ACT = mybir.ActivationFunctionType

P = 128
F = 8192
N_X = 512
N_REF = 1024
C = 128
EPS = 1e-8
PACK = 4
RUN = 128
PASSES = F // (PACK * RUN)
ROWS_Q = P // PACK
W_Q = F // PACK
NQ = (N_X + N_REF) // ROWS_Q
NQ_X = N_X // ROWS_Q
GROUPS = NQ // 4
GROUPS_X = NQ_X // 4
PF = 5


def tile_quantumkernelpca_kernel(tc, x, x_ref, mean_, components_, out):
    nc = tc.nc
    with ExitStack() as ctx:
        const = ctx.enter_context(tc.tile_pool(name="const", bufs=1))
        xin_pool = ctx.enter_context(tc.tile_pool(name="xin", bufs=PF + 1))
        d_pool = ctx.enter_context(tc.tile_pool(name="d", bufs=7))
        s_pool = ctx.enter_context(tc.tile_pool(name="s", bufs=3))
        grp_pool = ctx.enter_context(tc.tile_pool(name="grp", bufs=2))
        ref_pool = ctx.enter_context(tc.tile_pool(name="ref", bufs=2))
        small = ctx.enter_context(tc.tile_pool(name="small", bufs=4))
        psum_m = ctx.enter_context(tc.psum_pool(name="psum_m", bufs=1))
        psum_t = ctx.enter_context(tc.psum_pool(name="psum_t", bufs=3))
        psum_o = ctx.enter_context(tc.psum_pool(name="psum_o", bufs=2))
        psum_x = ctx.enter_context(tc.psum_pool(name="psum_x", bufs=1))
        if PIN:
            ctx.enter_context(tc.manual_schedule())

        mrows = const.tile([P, W_Q], BF16, name="mrows")
        mean_runs = mean_.rearrange("(g t f) -> t g f", t=PACK, f=RUN)
        for t in range(PACK):
            nc.sync.dma_start(
                out=mrows[t:ROWS_Q:PACK, :].rearrange("p (g f) -> p g f", f=RUN),
                in_=mean_runs[t].partition_broadcast(ROWS_Q // PACK),
            )
        nc.vector.memset(mrows[ROWS_Q:2 * ROWS_Q, :].bitcast(F32), 0.0)
        nc.vector.memset(mrows[2 * ROWS_Q:P, :].bitcast(F32), 0.0)
        tiny = const.tile([P, 1], F32, name="tiny")
        nc.vector.memset(tiny[:], 1e-30)
        warm = const.tile([P, 1], F32, name="warm")
        nc.scalar.activation(out=warm[:], in_=tiny[:], func=ACT.Sqrt)

        ident = const.tile([P, P], BF16, name="ident")
        make_identity(nc, ident[:])
        sel = const.tile([P, ROWS_Q, PACK], BF16, name="sel")
        nc.vector.tensor_copy(out=sel[:], in_=ident[:, 0:PACK].unsqueeze(1).to_broadcast([P, ROWS_Q, PACK]))
        spread = const.tile([P, ROWS_Q, PACK], BF16, name="spread")
        nc.vector.tensor_copy(out=spread[:], in_=ident[:, 0:ROWS_Q].unsqueeze(2).to_broadcast([P, ROWS_Q, PACK]))

        same_ps = psum_x.tile([P, P], F32, name="same_ps", tag="x")
        nc.tensor.matmul(
            out=same_ps[:],
            lhsT=spread[:].rearrange("p r t -> p (r t)"),
            rhs=spread[:].rearrange("p r t -> p (r t)"),
            start=True,
            stop=True,
        )
        mean_ps = []
        for h in range(2):
            mp = psum_m.tile([P, 1024], BF16, name="mean_ps%d" % h)
            for j in range(2):
                nc.tensor.matmul(
                    out=mp[:, j * 512:(j + 1) * 512],
                    lhsT=sel[:].rearrange("p r t -> p (r t)"),
                    rhs=mrows[:, (2 * h + j) * 512:(2 * h + j + 1) * 512],
                    start=True,
                    stop=True,
                )
            mean_ps.append(mp)
        same = const.tile([P, P], F32, name="same")

        junk = const.tile([P, W_Q], BF16, name="junk")
        x_codes = const.tile([P, PASSES, N_X], U32, name="x_codes", align_bytes=64)
        x_scales = const.tile([P, PASSES, N_X], U8, name="x_scales", align_bytes=64)
        comp_sb = const.tile([P, N_REF], BF16, name="comp_sb")
        comp_grp = const.tile([P, 2, C, PACK], BF16, name="comp_grp", align_bytes=64)
        comp_codes = const.tile([P, 2 * C], U32, name="comp_codes", align_bytes=64)
        comp_scales = const.tile([P, 2 * C], U8, name="comp_scales", align_bytes=64)
        k_planes = [const.tile([P, PACK, N_X], BF16, name="k_planes%d" % g2) for g2 in range(2)]
        k_grp = [const.tile([P, N_X, PACK], BF16, name="k_grp%d" % g2, align_bytes=64) for g2 in range(2)]
        k_codes = [const.tile([P, N_X], U32, name="k_codes%d" % g2, align_bytes=64) for g2 in range(2)]
        k_scales = [const.tile([P, N_X], U8, name="k_scales%d" % g2, align_bytes=64) for g2 in range(2)]

        xin = {}
        dif = {}
        acc = {}
        n2 = {}
        nrm = {}
        rinv = {}
        sn = {}
        tps = {}
        grp = {}
        rcodes = {}
        rscales = {}
        ov = {}
        ovs = {}
        res_ps = []

        def load(n):
            src = x if n < NQ_X else x_ref
            r0 = ROWS_Q * (n if n < NQ_X else n - NQ_X)
            t_in = xin_pool.tile([P, W_Q], BF16, name="xin", tag="xin")
            view = src[r0:r0 + ROWS_Q, :].rearrange("r (g w) -> r g w", w=PACK * RUN)
            for t in range(PACK):
                nc.sync.dma_start(
                    out=t_in[t:P:PACK, :].rearrange("p (g f) -> p g f", f=RUN),
                    in_=view[:, :, t * RUN:(t + 1) * RUN],
                )
            xin[n] = t_in

        def sub(n):
            t_d = d_pool.tile([P, W_Q], F32, name="dif", tag="dif")
            for h in range(2):
                nc.vector.tensor_tensor(
                    out=t_d[:, h * 1024:(h + 1) * 1024],
                    in0=xin[n][:, h * 1024:(h + 1) * 1024],
                    in1=mean_ps[h][:],
                    op=ALU.subtract,
                )
            dif[n] = t_d

        def square(n):
            p2 = n // 2
            if n % 2 == 0:
                acc[p2] = small.tile([P, 2], F32, name="acc", tag="acc")
            nc.scalar.activation(out=junk[:], in_=dif[n][:], func=ACT.Square, accum_out=acc[p2][:, n % 2:n % 2 + 1])

        def norm_sum(p2):
            n2[p2] = psum_x.tile([P, 2], F32, name="n2", tag="x")
            nc.tensor.matmul(out=n2[p2][:], lhsT=same[:], rhs=acc[p2][:], start=True, stop=True)

        def norm_sqrt(p2):
            nrm[p2] = small.tile([P, 2], F32, name="nrm", tag="nrm")
            nc.scalar.activation(out=nrm[p2][:], in_=n2[p2][:], func=ACT.Sqrt, bias=tiny[:])

        def norm_recip(p2):
            ne = small.tile([P, 2], F32, name="ne", tag="ne")
            nc.vector.tensor_scalar_add(out=ne[:], in0=nrm[p2][:], scalar1=EPS)
            rinv[p2] = small.tile([P, 2], F32, name="rinv", tag="rinv")
            nc.vector.reciprocal(out=rinv[p2][:], in_=ne[:])

        def scale(n):
            t_s = s_pool.tile([P, W_Q], BF16, name="sn", tag="sn")
            r = rinv[n // 2][:, n % 2:n % 2 + 1]
            if SCALE_RULE == "g" and n < NQ - 4:
                nc.gpsimd.tensor_scalar(out=t_s[:], in0=dif[n][:], scalar1=r, scalar2=0.0, op0=ALU.mult, op1=ALU.add)
            elif True:
                nc.vector.tensor_scalar(out=t_s[:], in0=dif[n][:], scalar1=r, scalar2=None, op0=ALU.mult)
            else:
                nc.scalar.activation(out=t_s[:], in_=dif[n][:], func=ACT.Copy, scale=r)
            sn[n] = t_s

        def transposes(n):
            for hb in range(2):
                tp = psum_t.tile([P, 8, P], BF16, name="tp", tag="tp")
                for gg in range(8):
                    g = 8 * hb + gg
                    nc.tensor.transpose(tp[:, gg, :], sn[n][:, g * RUN:(g + 1) * RUN], ident[:])
                tps[(n, hb)] = tp

        def evacuate(n):
            a = n // 4
            q = n % 4
            if q == 0:
                grp[a] = grp_pool.tile([P, PASSES, PACK * P], BF16, name="grp", tag="grp", align_bytes=64)
            for hb in range(2):
                dst = grp[a][:, 8 * hb:8 * hb + 8, q * P:(q + 1) * P]
                if EVAC_V_EVERY and (2 * n + hb) % EVAC_V_EVERY == 0:
                    nc.vector.tensor_copy(out=dst, in_=tps[(n, hb)][:])
                else:
                    nc.scalar.copy(out=dst, in_=tps[(n, hb)][:])

        def quantise(a, c):
            if a < GROUPS_X:
                for g in range(4 * c, 4 * c + 4):
                    nc.vector.quantize_mx(
                        out=x_codes[:, g, a * P:(a + 1) * P].bitcast(FP8X4),
                        scales=x_scales[:, g, a * P:(a + 1) * P],
                        in_=grp[a][:, g, :],
                    )
            else:
                if c == 0:
                    rcodes[a] = ref_pool.tile([P, PASSES * P], U32, name="rcodes", tag="rcodes", align_bytes=64)
                    rscales[a] = ref_pool.tile([P, PASSES * P], U8, name="rscales", tag="rscales", align_bytes=64)
                nc.vector.quantize_mx(
                    out=rcodes[a][:, c * 512:(c + 1) * 512].bitcast(FP8X4),
                    scales=rscales[a][:, c * 512:(c + 1) * 512],
                    in_=grp[a][:, 4 * c:4 * c + 4, :].rearrange("p g w -> p (g w)"),
                )

        def overlap(a, c):
            if c == 0:
                ov[a] = psum_o.tile([P, N_X], F32, name="ov", tag="ov")
            for g in range(4 * c, 4 * c + 4):
                nc.tensor.matmul_mx(
                    out=ov[a][:],
                    lhsT=rcodes[a][:, g * P:(g + 1) * P].bitcast(FP8X4),
                    lhsT_scale=rscales[a][:, g * P:(g + 1) * P],
                    rhs=x_codes[:, g, :].bitcast(FP8X4),
                    rhs_scale=x_scales[:, g, :],
                    start=(g == 0),
                    stop=(g == PASSES - 1),
                )

        def fidelity(a):
            j = a - GROUPS_X
            if j >= 6:
                nc.scalar.activation(out=k_grp[1][:, :, j % 4], in_=ov[a][:], func=ACT.Square)
            else:
                nc.scalar.activation(out=k_planes[j // 4][:, j % 4, :], in_=ov[a][:], func=ACT.Square)

        def fidelity_copy(a):
            ovs[a] = small.tile([P, N_X], F32, name="ovs", tag="ovs")
            nc.vector.tensor_copy(out=ovs[a][:], in_=ov[a][:])

        def fidelity_mult(a):
            j = a - GROUPS_X
            nc.vector.tensor_tensor(out=k_planes[j // 4][:, j % 4, :], in0=ovs[a][:], in1=ov[a][:], op=ALU.mult)

        def lay_k(g2, planes):
            nc.vector.tensor_copy(
                out=k_grp[g2][:, :, 0:planes], in_=k_planes[g2][:, 0:planes, :].rearrange("p t i -> p i t")
            )

        def quantise_k(g2):
            nc.vector.quantize_mx(
                out=k_codes[g2][:].bitcast(FP8X4),
                scales=k_scales[g2][:],
                in_=k_grp[g2][:].rearrange("p i t -> p (i t)"),
            )

        def project(it, g2):
            if g2 == 0:
                pool = psum_t if it < 3 else psum_x
                res_ps.append(pool.tile([P, C], F32, name="res_ps", tag="tp" if it < 3 else "x"))
            nc.tensor.matmul_mx(
                out=res_ps[it][:],
                lhsT=k_codes[g2][:, it * P:(it + 1) * P].bitcast(FP8X4),
                lhsT_scale=k_scales[g2][:, it * P:(it + 1) * P],
                rhs=comp_codes[:, g2 * C:(g2 + 1) * C].bitcast(FP8X4),
                rhs_scale=comp_scales[:, g2 * C:(g2 + 1) * C],
                start=(g2 == 0),
                stop=(g2 == 1),
            )

        def components_load():
            nc.sync.dma_start(out=comp_sb[:], in_=components_)

        def components_transposes():
            ctp = psum_x.tile([P, 8, C], BF16, name="ctp", tag="x")
            for b in range(8):
                nc.tensor.transpose(ctp[:, b, :], comp_sb[:, b * RUN:(b + 1) * RUN], ident[:])
            return ctp

        def components_quantise(ctp):
            nc.vector.tensor_copy(out=comp_grp[:], in_=ctp[:].rearrange("p (g t) c -> p g c t", t=PACK))
            nc.vector.quantize_mx(
                out=comp_codes[:].bitcast(FP8X4),
                scales=comp_scales[:],
                in_=comp_grp[:].rearrange("p g c t -> p (g c t)"),
            )

        for n in range(PF):
            load(n)
        last_step = 4 * (GROUPS - 1) + 14
        for n in range(last_step + 1):
            if n + PF < NQ:
                load(n + PF)
            if n == 8:
                components_load()
            if n < NQ:
                sub(n)
                square(n)
            if n == 0:
                nc.vector.tensor_copy(out=same[:], in_=same_ps[:])
            if n >= 2 and n % 2 == 0 and (n - 2) // 2 < NQ // 2:
                norm_sum((n - 2) // 2)
                norm_sqrt((n - 2) // 2)
            if n >= 3 and n % 2 == 1 and (n - 3) // 2 < NQ // 2:
                norm_recip((n - 3) // 2)
            if n == 49:
                comp_ps = components_transposes()
            if n == 51:
                components_quantise(comp_ps)
            if 0 <= n - 4 < NQ:
                scale(n - 4)
            if 0 <= n - 5 < NQ:
                transposes(n - 5)
                evacuate(n - 5)
            if n >= 9 and (n - 9) // 4 < GROUPS:
                quantise((n - 9) // 4, (n - 9) % 4)
            if n >= 14 + 4 * GROUPS_X and (n - 14) % 4 == 0 and (n - 14) // 4 < 10:
                fidelity_copy((n - 14) // 4)
            if n >= 16 + 4 * GROUPS_X and (n - 16) % 4 == 0 and (n - 16) // 4 < 10:
                fidelity_mult((n - 16) // 4)
            if n >= 9 + 4 * GROUPS_X and (n - 9) // 4 < GROUPS:
                overlap((n - 9) // 4, (n - 9) % 4)
            if n >= 13 + 4 * GROUPS_X and (n - 13) % 4 == 0 and 10 <= (n - 13) // 4 < GROUPS:
                fidelity((n - 13) // 4)
            if n == 53:
                for it in range(4):
                    project(it, 0)
            if n == 52:
                lay_k(0, PACK)
                lay_k(1, 2)
                quantise_k(0)
        quantise_k(1)
        for it in range(4):
            project(it, 1)
        res = const.tile([P, 4, C], F32, name="res")
        out_view = out.rearrange("(a p) c -> p a c", p=P)
        for it in range(2):
            nc.vector.tensor_copy(out=res[:, it, :], in_=res_ps[it][:])
            nc.scalar.copy(out=res[:, it + 2, :], in_=res_ps[it + 2][:])
        nc.sync.dma_start(out=out_view[:, 0:2, :], in_=res[:, 0:2, :])
        nc.scalar.dma_start(out=out_view[:, 2:4, :], in_=res[:, 2:4, :])
